import numpy as np
import ml_dtypes


def mxq(x, axis, fmt="e4m3"):
    dtype, down = {"e4m3": (ml_dtypes.float8_e4m3fn, 7), "e5m2": (ml_dtypes.float8_e5m2, 14)}[fmt]
    v = np.moveaxis(np.asarray(x, np.float32).astype(ml_dtypes.bfloat16).astype(np.float64), axis, -1)
    blocks = v.reshape(v.shape[:-1] + (-1, 32))
    amax = np.abs(blocks).max(-1, keepdims=True)
    byte = np.maximum(np.where(amax > 0, np.frexp(amax)[1] - 1 + 127, 0) - down, 1)
    scale = np.exp2(byte - 127.0)
    codes = (blocks / scale).astype(np.float32).astype(dtype).astype(np.float64)
    return np.moveaxis((codes * scale).reshape(v.shape), -1, axis)


WIDE = False


def mx_kscale(k):
    if not WIDE:
        return np.ones(k)
    levels = np.array([10, -10, 5, -5, 0])
    if k % 512:
        return np.exp2(np.random.permutation(np.resize(levels, k // 32))).repeat(32)
    a = np.empty((k // 512, 16))
    for p in range(k // 512):
        a[p, :8] = np.random.permutation(np.resize(levels, 8))
        for g in range(8):
            far = levels[np.abs(levels - a[p, g]) >= 10]
            a[p, g + 8] = far[np.random.randint(len(far))]
    return np.exp2(a.ravel()).repeat(32)


BF16 = ml_dtypes.bfloat16


def bf(x):
    return np.asarray(x, np.float32).astype(BF16)


def f64(x):
    return np.asarray(x).astype(np.float64)


B, T, C, NH, NC = 2, 2048, 512, 4, 2
HS = C // NH
N = T // NC


def draw0():
    s = mx_kscale(C)
    t = mx_kscale(T)
    return {"x": bf(np.random.standard_normal((B, T, C)) * s * t[:, None]),
            "Wk": bf(np.random.standard_normal((C, C)) / np.sqrt(C) / s),
            "pk_W": bf(np.random.standard_normal((NC, N, N)) / np.sqrt(N) / t.reshape(NC, 1, N)),
            "pk_b": bf(np.random.standard_normal((NC, N)) * 0.3)}


def core(x, Wk, pk_W, pk_b):
    kh = mxq(f64(x), 2, "e4m3") @ mxq(f64(Wk), 1, "e4m3").T
    kh = kh.reshape(B, T, NH, HS).transpose(0, 2, 1, 3).reshape(B, NH, NC, N, HS)
    out = (mxq(f64(pk_W), 2, "e4m3") @ mxq(kh, 3, "e4m3")) + f64(pk_b)[:, :, None]
    return out.reshape(B, NH, T, HS)


def e4m3fn_bytes(y):
    return np.clip(np.asarray(y, np.float64), -448.0, 448.0).astype(np.float32).astype(ml_dtypes.float8_e4m3fn).view(np.uint8)


def e4m3fn_values(b):
    return np.asarray(b, np.uint8).view(ml_dtypes.float8_e4m3fn).astype(np.float64)


def setup_inputs():
    d = draw0()
    x0 = np.asarray(d['Wk']).astype(np.float64)
    s = (np.max(np.abs(x0), axis=(0,), keepdims=True) / 448.0).astype(np.float32)
    out = {}
    for k, v in d.items():
        if k == 'Wk':
            out['Wk_bytes'] = e4m3fn_bytes(x0 / s.astype(np.float64))
            out['Wk_scale'] = s
        else:
            out[k] = v
    return out


def reference(x, Wk_bytes, Wk_scale, pk_W, pk_b):
    return core(x, e4m3fn_values(Wk_bytes) * Wk_scale.astype(np.float64), pk_W, pk_b)

@@ -1,0 +1,304 @@
+from contextlib import ExitStack
+
+import concourse.mybir as mybir
+from concourse.masks import make_identity
+
+B, T, C, NH, NC = 2, 2048, 512, 4, 2
+D = C // NH
+N = T // NC
+FLOPS = 2 * B * T * C * C + 2 * B * T * N * C
+
+F32 = mybir.dt.float32
+BF16 = mybir.dt.bfloat16
+U32 = mybir.dt.uint32
+U8 = mybir.dt.uint8
+FP8 = mybir.dt.float8_e4m3fn
+FP8X4 = mybir.dt.float8_e4m3fn_x4
+ADD = mybir.AluOpType.add
+MULT = mybir.AluOpType.mult
+IDENT = mybir.ActivationFunctionType.Identity
+P = 128
+
+EVAC = "SVS"
+QDELAY = 2
+LEAD = 4
+DEINT_X = []
+DEINT_P = []
+DEINT_ENGINE = "V"
+
+
+def build_schedule():
+    def xj(i):
+        return [("X", i, 0), ("X", i, 1)]
+
+    def pj(c, js):
+        return [("P", c, j) for j in js]
+
+    def sj(i):
+        return [("S", i, h) for h in range(4)]
+
+    def oj(pair, js):
+        return [("O", pair, j) for j in js]
+
+    w = [("W", 0, 0), ("W", 1, 0)]
+    return (
+        xj(0) + w + xj(1) + xj(2) + pj(0, [0, 1]) + sj(0)
+        + pj(0, [2, 3]) + pj(0, [4, 5]) + sj(1) + xj(3) + pj(0, [6, 7]) + sj(2)
+        + xj(4) + pj(1, [0, 1]) + oj(0, [0, 1]) + oj(0, [2, 3]) + sj(3) + xj(5)
+        + pj(1, [2, 3]) + oj(0, [4, 5]) + oj(0, [6, 7]) + sj(4) + xj(6) + pj(1, [4, 5])
+        + oj(1, [0, 1]) + oj(1, [2, 3]) + sj(5) + xj(7) + pj(1, [6, 7]) + oj(1, [4, 5])
+        + oj(1, [6, 7]) + sj(6) + oj(2, [0, 1]) + oj(2, [2, 3]) + sj(7) + oj(2, [4, 5])
+        + oj(2, [6, 7]) + oj(3, [0, 1]) + oj(3, [2, 3]) + oj(3, [4, 5]) + oj(3, [6, 7])
+    )
+
+
+def tile_causalselfattention_pa_t_kernel(tc, x, wk_bytes, wk_scale, pk_w, pk_b, out):
+    nc = tc.nc
+    with ExitStack() as ctx:
+        keep = ctx.enter_context(tc.tile_pool(name="keep", bufs=1))
+        work = ctx.enter_context(tc.tile_pool(name="work", bufs=3))
+        psum = ctx.enter_context(tc.psum_pool(name="psum", bufs=8))
+        ctx.enter_context(tc.manual_schedule())
+
+        wb = keep.tile([P, 4, C], U8, name="wb", align_bytes=64)
+        nc.sync.dma_start(out=wb[:], in_=wk_bytes.rearrange("(i r) k -> r i k", r=P))
+        ws = keep.tile([P, 4], F32, name="ws", align_bytes=64)
+        nc.scalar.dma_start(out=ws[:], in_=wk_scale.rearrange("o (p t) -> p (o t)", t=4))
+
+        xraw = {}
+        praw = {}
+
+        def load_x(i, pieces):
+            pair, u = divmod(i, 2)
+            c, b = divmod(pair, 2)
+            r0 = c * N + u * 512
+            t = keep.tile([P, 4, C], BF16, name="xraw%d" % i, align_bytes=64)
+            src = x[b, r0:r0 + 512, :].rearrange("(m t) k -> m t k", t=4)
+            n = 4 // pieces
+            for s in range(pieces):
+                nc.sync.dma_start(out=t[:, s * n:(s + 1) * n, :], in_=src[:, s * n:(s + 1) * n, :])
+            xraw[i] = t
+
+        def load_p(c, q, half):
+            if (c, q) not in praw:
+                praw[(c, q)] = keep.tile([P, 4, N], BF16, name="praw%d%d" % (c, q), align_bytes=64)
+            src = pk_w[c, q * 512:(q + 1) * 512, :].rearrange("(m j) k -> m j k", j=4)
+            rows = slice(2 * half, 2 * half + 2)
+            nc.sync.dma_start(out=praw[(c, q)][:, rows, :], in_=src[:, rows, :])
+
+        load_x(0, 2)
+        bias_bf = keep.tile([P, 4, 4], BF16, name="bias_bf", align_bytes=64)
+        bias = keep.tile([P, 16], F32, name="bias", align_bytes=64)
+        load_x(1, 1)
+        load_x(2, 1)
+        nc.sync.dma_start(out=bias_bf[:], in_=pk_b.rearrange("c (q p j) -> p (c q) j", q=2, j=4))
+        load_p(0, 0, 0)
+        load_p(0, 0, 1)
+        load_p(0, 1, 0)
+        load_x(3, 1)
+        load_p(0, 1, 1)
+        load_x(4, 1)
+        load_p(1, 0, 0)
+        load_x(5, 1)
+        load_p(1, 0, 1)
+        load_x(6, 1)
+        load_p(1, 1, 0)
+        load_x(7, 1)
+        load_p(1, 1, 1)
+
+        warm = keep.tile([P, 1], F32, name="warm")
+        warm2 = keep.tile([P, 1], F32, name="warm2")
+        nc.vector.memset(warm[:], 0.0)
+        nc.scalar.activation(out=warm2[:], in_=warm[:], func=IDENT)
+        ident = keep.tile([P, P], F32, name="ident", align_bytes=64)
+        make_identity(nc, ident[:])
+        ident_bf = keep.tile([P, P], BF16, name="ident_bf", align_bytes=64)
+        nc.gpsimd.tensor_copy(out=ident_bf[:], in_=ident[:])
+        nc.gpsimd.tensor_copy(out=bias[:], in_=bias_bf[:].rearrange("p a j -> p (a j)"))
+
+        wv = keep.tile([P, 4, C], BF16, name="wv", align_bytes=64)
+        nc.vector.tensor_copy(out=wv[:, 0:2, :].rearrange("p i k -> p (i k)"),
+                              in_=wb[:, 0:2, :].rearrange("p i k -> p (i k)").bitcast(FP8))
+        nc.scalar.copy(out=wv[:, 2:4, :].rearrange("p i k -> p (i k)"),
+                       in_=wb[:, 2:4, :].rearrange("p i k -> p (i k)").bitcast(FP8))
+
+        wg = keep.tile([P, C * 4], BF16, name="wg", align_bytes=64)
+        wcodes = keep.tile([P, C], U32, name="wcodes", align_bytes=64)
+        wscales = keep.tile([P, C], U8, name="wscales", align_bytes=64)
+
+        xcodes, xscales, pcodes, pscales, kcodes, kscales, otiles = {}, {}, {}, {}, {}, {}, {}
+        grouped = {}
+        due = []
+        count = [0, 0]
+        words = {}
+
+        def evac_engine():
+            e = EVAC[count[1] % len(EVAC)]
+            count[1] += 1
+            return e
+
+        def copy_out(out_, in_):
+            if evac_engine() == "S":
+                nc.scalar.copy(out=out_, in_=in_)
+            else:
+                nc.vector.tensor_copy(out=out_, in_=in_)
+
+        def later(fn):
+            due.append((count[0] + QDELAY, fn))
+
+        def quant(codes, scales, src):
+            nc.vector.quantize_mx(out=codes[:].bitcast(FP8X4), scales=scales[:], in_=src[:])
+
+        def raw_words(kind, i, a):
+            if kind == "X":
+                return xraw[i][:, 2 * a:2 * a + 2, :].rearrange("p s k -> p (s k)").bitcast(F32)
+            return praw[(i, a // 4)][:, a % 4, :].bitcast(F32)
+
+        def deinterleave(job):
+            kind = job[0]
+            if job in words:
+                return
+            if (kind == "X" and job[1] in DEINT_X) or (kind == "P" and (job[1] * 8 + job[2]) in DEINT_P):
+                d = work.tile([P, 4, P], F32, name="deint", bufs=6, align_bytes=64)
+                eng = nc.vector if DEINT_ENGINE == "V" else nc.gpsimd
+                eng.tensor_copy(out=d[:].rearrange("p (g u) m -> p g u m", g=2),
+                                in_=raw_words(*job).rearrange("p (g m u) -> p g u m", g=2, u=2))
+                words[job] = [d[:, n, :] for n in range(4)]
+            elif kind in ("X", "P"):
+                r = raw_words(*job)
+                words[job] = [r[:, 256 * g + u:256 * (g + 1):2] for g in range(2) for u in range(2)]
+
+        def bank(name):
+            return psum.tile([P, 512], F32, name="bank")
+
+        def turn(job, dst):
+            bk = bank("t")
+            for n in range(4):
+                nc.tensor.transpose(bk[:, n * P:(n + 1) * P], words[job][n], ident[:])
+            copy_out(dst.bitcast(F32).rearrange("p (g m u) -> p g m u", g=2, u=2),
+                     bk[:].rearrange("p (g u m) -> p g m u", g=2, u=2))
+
+        def do_w(a):
+            bk = psum.tile([P, 2, 4, P], BF16, name="bank")
+            for i2 in range(2):
+                for t in range(4):
+                    nc.tensor.transpose(bk[:, i2, t, :], wv[:, 2 * a + i2, t:C:4], ident_bf[:])
+            for i2 in range(2):
+                base = (2 * a + i2) * 512
+                nc.vector.tensor_tensor(
+                    out=wg[:, base:base + 512].rearrange("p (r t) -> p r t", t=4),
+                    in0=bk[:, i2, :, :].rearrange("p t r -> p r t"),
+                    in1=ws[:].unsqueeze(1).to_broadcast([P, P, 4]),
+                    op=MULT)
+            if a == 1:
+                later(lambda: quant(wcodes, wscales, wg))
+
+        def do_x(i, a):
+            if a == 0:
+                grouped[("X", i)] = work.tile([P, 2048], BF16, name="xg", align_bytes=64)
+            g = grouped[("X", i)]
+            turn(("X", i, a), g[:, a * 1024:(a + 1) * 1024])
+            if a == 1:
+                xcodes[i] = work.tile([P, C], U32, name="xcodes", bufs=4, align_bytes=64)
+                xscales[i] = work.tile([P, C], U8, name="xscales", bufs=4, align_bytes=64)
+                later(lambda: quant(xcodes[i], xscales[i], g))
+
+        def do_p(c, j):
+            key = (c, j // 2)
+            if j % 2 == 0:
+                grouped[("P",) + key] = work.tile([P, 2048], BF16, name="pg", align_bytes=64)
+            g = grouped[("P",) + key]
+            turn(("P", c, j), g[:, (j % 2) * 1024:(j % 2 + 1) * 1024])
+            if j % 2 == 1:
+                pcodes[key] = keep.tile([P, 512], U32, name="pcodes%d%d" % key, align_bytes=64)
+                pscales[key] = keep.tile([P, 512], U8, name="pscales%d%d" % key, align_bytes=64)
+                later(lambda: quant(pcodes[key], pscales[key], g))
+
+        def do_s(i, h):
+            if h == 0:
+                grouped[("K", i)] = work.tile([P, 2048], BF16, name="kg", align_bytes=64)
+            g = grouped[("K", i)]
+            bk = bank("s")
+            for t in range(4):
+                nc.tensor.matmul_mx(
+                    out=bk[:, t * P:(t + 1) * P],
+                    lhsT=xcodes[i][:, t * P:(t + 1) * P].bitcast(FP8X4),
+                    lhsT_scale=xscales[i][:, t * P:(t + 1) * P],
+                    rhs=wcodes[:, h * P:(h + 1) * P].bitcast(FP8X4),
+                    rhs_scale=wscales[:, h * P:(h + 1) * P],
+                    start=True, stop=True)
+            copy_out(g[:, h * 512:(h + 1) * 512].rearrange("p (n t) -> p n t", t=4),
+                     bk[:].rearrange("p (t n) -> p n t", t=4))
+            if h == 3:
+                kcodes[i] = work.tile([P, C], U32, name="kcodes", bufs=8, align_bytes=64)
+                kscales[i] = work.tile([P, C], U8, name="kscales", bufs=8, align_bytes=64)
+                later(lambda: quant(kcodes[i], kscales[i], g))
+
+        def do_o(pair, j):
+            c, b = divmod(pair, 2)
+            q, jj = divmod(j, 4)
+            if jj == 0:
+                otiles[(pair, q)] = work.tile([P, NH, 4, D], F32, name="o", align_bytes=64)
+            o = otiles[(pair, q)]
+            bk = bank("o")
+            s0 = (j % 2) * 256
+            key = (c, j // 2)
+            for u in range(2):
+                cols = slice(s0 + u * P, s0 + (u + 1) * P)
+                nc.tensor.matmul_mx(
+                    out=bk[:],
+                    lhsT=pcodes[key][:, cols].bitcast(FP8X4),
+                    lhsT_scale=pscales[key][:, cols],
+                    rhs=kcodes[2 * pair + u][:].bitcast(FP8X4),
+                    rhs_scale=kscales[2 * pair + u][:],
+                    start=(u == 0), stop=(u == 1))
+            bcol = bias[:, (2 * c + q) * 4 + jj:(2 * c + q) * 4 + jj + 1]
+            src = bk[:].rearrange("p (h d) -> p h d", h=NH)
+            last = pair == 3 and j == 7
+
+            def emit(e, h0, h1):
+                if e == "S":
+                    nc.scalar.activation(out=o[:, h0:h1, jj, :], in_=src[:, h0:h1, :], func=IDENT, bias=bcol)
+                else:
+                    nc.vector.tensor_scalar(out=o[:, h0:h1, jj, :], in0=src[:, h0:h1, :], scalar1=bcol, scalar2=None, op0=ADD)
+
+            r0 = c * N + q * 512
+
+            def store(eng, h0, h1, j0, j1):
+                dst = out[b, h0:h1, r0:r0 + 512, :].rearrange("h (p j) d -> p h j d", j=4)[:, :, j0:j1, :]
+                eng.dma_start(out=dst.rearrange("p h j d -> p h (j d)"),
+                              in_=o[:, h0:h1, j0:j1, :].rearrange("p h j d -> p h (j d)"))
+
+            if last:
+                emit("V", 0, 2)
+                emit("S", 2, 4)
+                store(nc.sync, 0, 2, jj, 4)
+                store(nc.scalar, 2, 4, jj, 4)
+            else:
+                emit(evac_engine(), 0, NH)
+                if pair == 3 and q == 1:
+                    if jj == 1:
+                        store(nc.sync, 0, NH, 0, 2)
+                    elif jj == 2:
+                        store(nc.sync, 0, NH, 2, 3)
+                elif jj == 3:
+                    store(nc.sync, 0, NH, 0, 4)
+
+        schedule = build_schedule()
+        for n, job in enumerate(schedule):
+            for ahead in schedule[n:n + LEAD + 1]:
+                deinterleave(ahead)
+            kind = job[0]
+            if kind == "W":
+                do_w(job[1])
+            elif kind == "X":
+                do_x(job[1], job[2])
+            elif kind == "P":
+                do_p(job[1], job[2])
+            elif kind == "S":
+                do_s(job[1], job[2])
+            else:
+                do_o(job[1], job[2])
+            count[0] += 1
+            while due and due[0][0] <= count[0]:
+                due.pop(0)[1]()

@@ -19,11 +19,11 @@ MULT = mybir.AluOpType.mult
 IDENT = mybir.ActivationFunctionType.Identity
 P = 128
 
-EVAC = "SVS"
-QDELAY = 2
-LEAD = 4
-DEINT_X = []
-DEINT_P = []
+EVAC = "SSVSSSV"
+QDELAY = 3
+LEAD = 10
+DEINT_X = [6,7]
+DEINT_P = [6,7,8,9,10,11,12,13,14,15]
 DEINT_ENGINE = "V"
 
 
@@ -34,21 +34,23 @@ def build_schedule():
     def pj(c, js):
         return [("P", c, j) for j in js]
 
-    def sj(i):
-        return [("S", i, h) for h in range(4)]
+    def sj(i, hs=(0, 1, 2, 3)):
+        return [("S", i, h) for h in hs]
 
     def oj(pair, js):
         return [("O", pair, j) for j in js]
 
     w = [("W", 0, 0), ("W", 1, 0)]
     return (
-        xj(0) + w + xj(1) + xj(2) + pj(0, [0, 1]) + sj(0)
-        + pj(0, [2, 3]) + pj(0, [4, 5]) + sj(1) + xj(3) + pj(0, [6, 7]) + sj(2)
-        + xj(4) + pj(1, [0, 1]) + oj(0, [0, 1]) + oj(0, [2, 3]) + sj(3) + xj(5)
-        + pj(1, [2, 3]) + oj(0, [4, 5]) + oj(0, [6, 7]) + sj(4) + xj(6) + pj(1, [4, 5])
-        + oj(1, [0, 1]) + oj(1, [2, 3]) + sj(5) + xj(7) + pj(1, [6, 7]) + oj(1, [4, 5])
-        + oj(1, [6, 7]) + sj(6) + oj(2, [0, 1]) + oj(2, [2, 3]) + sj(7) + oj(2, [4, 5])
-        + oj(2, [6, 7]) + oj(3, [0, 1]) + oj(3, [2, 3]) + oj(3, [4, 5]) + oj(3, [6, 7])
+        xj(0) + w + pj(0, [0, 1]) + xj(1) + xj(2) + xj(3)
+        + pj(0, [2, 3]) + pj(0, [4, 5]) + xj(4) + sj(0, [0, 1]) + sj(0, [2, 3]) + sj(1, [0, 1])
+        + sj(1, [2, 3]) + xj(5) + sj(2, [0, 1]) + xj(6) + oj(0, [0, 1]) + sj(2, [2, 3])
+        + sj(3, [0, 1]) + oj(0, [2, 3]) + pj(0, [6, 7]) + pj(1, [0, 1]) + oj(0, [4, 5]) + sj(3, [2, 3])
+        + sj(4, [0, 1]) + sj(4, [2, 3]) + oj(0, [6, 7]) + sj(5, [0, 1]) + sj(5, [2, 3]) + sj(6, [0, 1])
+        + oj(1, [0, 1]) + oj(1, [2, 3]) + xj(7) + pj(1, [2, 3]) + sj(6, [2, 3]) + oj(1, [4, 5])
+        + pj(1, [4, 5]) + oj(1, [6, 7]) + oj(2, [0, 1]) + oj(2, [2, 3]) + pj(1, [6, 7]) + sj(7, [0, 1])
+        + sj(7, [2, 3]) + oj(2, [4, 5]) + oj(2, [6, 7]) + oj(3, [0, 1]) + oj(3, [2, 3]) + oj(3, [4, 5])
+        + oj(3, [6, 7])
     )
 
 
@@ -89,21 +91,21 @@ def tile_causalselfattention_pa_t_kernel(tc, x, wk_bytes, wk_scale, pk_w, pk_b, 
         load_x(0, 2)
         bias_bf = keep.tile([P, 4, 4], BF16, name="bias_bf", align_bytes=64)
         bias = keep.tile([P, 16], F32, name="bias", align_bytes=64)
+        load_p(0, 0, 0)
         load_x(1, 1)
         load_x(2, 1)
-        nc.sync.dma_start(out=bias_bf[:], in_=pk_b.rearrange("c (q p j) -> p (c q) j", q=2, j=4))
-        load_p(0, 0, 0)
+        load_x(3, 1)
         load_p(0, 0, 1)
         load_p(0, 1, 0)
-        load_x(3, 1)
-        load_p(0, 1, 1)
         load_x(4, 1)
-        load_p(1, 0, 0)
         load_x(5, 1)
-        load_p(1, 0, 1)
         load_x(6, 1)
-        load_p(1, 1, 0)
+        load_p(0, 1, 1)
+        load_p(1, 0, 0)
+        nc.sync.dma_start(out=bias_bf[:], in_=pk_b.rearrange("c (q p j) -> p (c q) j", q=2, j=4))
         load_x(7, 1)
+        load_p(1, 0, 1)
+        load_p(1, 1, 0)
         load_p(1, 1, 1)
 
         warm = keep.tile([P, 1], F32, name="warm")
@@ -159,7 +161,7 @@ def tile_causalselfattention_pa_t_kernel(tc, x, wk_bytes, wk_scale, pk_w, pk_b, 
             if job in words:
                 return
             if (kind == "X" and job[1] in DEINT_X) or (kind == "P" and (job[1] * 8 + job[2]) in DEINT_P):
-                d = work.tile([P, 4, P], F32, name="deint", bufs=6, align_bytes=64)
+                d = work.tile([P, 4, P], F32, name="deint", bufs=10, align_bytes=64)
                 eng = nc.vector if DEINT_ENGINE == "V" else nc.gpsimd
                 eng.tensor_copy(out=d[:].rearrange("p (g u) m -> p g u m", g=2),
                                 in_=raw_words(*job).rearrange("p (g m u) -> p g u m", g=2, u=2))
@@ -199,8 +201,8 @@ def tile_causalselfattention_pa_t_kernel(tc, x, wk_bytes, wk_scale, pk_w, pk_b, 
             g = grouped[("X", i)]
             turn(("X", i, a), g[:, a * 1024:(a + 1) * 1024])
             if a == 1:
-                xcodes[i] = work.tile([P, C], U32, name="xcodes", bufs=4, align_bytes=64)
-                xscales[i] = work.tile([P, C], U8, name="xscales", bufs=4, align_bytes=64)
+                xcodes[i] = work.tile([P, C], U32, name="xcodes", bufs=6, align_bytes=64)
+                xscales[i] = work.tile([P, C], U8, name="xscales", bufs=6, align_bytes=64)
                 later(lambda: quant(xcodes[i], xscales[i], g))
 
         def do_p(c, j):
@@ -272,15 +274,13 @@ def tile_causalselfattention_pa_t_kernel(tc, x, wk_bytes, wk_scale, pk_w, pk_b, 
             if last:
                 emit("V", 0, 2)
                 emit("S", 2, 4)
-                store(nc.sync, 0, 2, jj, 4)
-                store(nc.scalar, 2, 4, jj, 4)
+                store(nc.sync, 0, 2, 2, 4)
+                store(nc.scalar, 2, 4, 2, 4)
             else:
                 emit(evac_engine(), 0, NH)
                 if pair == 3 and q == 1:
                     if jj == 1:
                         store(nc.sync, 0, NH, 0, 2)
-                    elif jj == 2:
-                        store(nc.sync, 0, NH, 2, 3)
                 elif jj == 3:
                     store(nc.sync, 0, NH, 0, 4)
 

@@ -19,11 +19,11 @@ MULT = mybir.AluOpType.mult
 IDENT = mybir.ActivationFunctionType.Identity
 P = 128
 
-EVAC = "SSVSSSV"
+EVAC = {"t": "SVS", "s": "SSSV", "o": "SSVSSSV"}
 QDELAY = 3
 LEAD = 10
 DEINT_X = [6,7]
-DEINT_P = [6,7,8,9,10,11,12,13,14,15]
+DEINT_P = [8,9,10,11,12,13,14,15]
 DEINT_ENGINE = "V"
 
 
@@ -42,14 +42,13 @@ def build_schedule():
 
     w = [("W", 0, 0), ("W", 1, 0)]
     return (
-        xj(0) + w + pj(0, [0, 1]) + xj(1) + xj(2) + xj(3)
-        + pj(0, [2, 3]) + pj(0, [4, 5]) + xj(4) + sj(0, [0, 1]) + sj(0, [2, 3]) + sj(1, [0, 1])
-        + sj(1, [2, 3]) + xj(5) + sj(2, [0, 1]) + xj(6) + oj(0, [0, 1]) + sj(2, [2, 3])
-        + sj(3, [0, 1]) + oj(0, [2, 3]) + pj(0, [6, 7]) + pj(1, [0, 1]) + oj(0, [4, 5]) + sj(3, [2, 3])
-        + sj(4, [0, 1]) + sj(4, [2, 3]) + oj(0, [6, 7]) + sj(5, [0, 1]) + sj(5, [2, 3]) + sj(6, [0, 1])
-        + oj(1, [0, 1]) + oj(1, [2, 3]) + xj(7) + pj(1, [2, 3]) + sj(6, [2, 3]) + oj(1, [4, 5])
-        + pj(1, [4, 5]) + oj(1, [6, 7]) + oj(2, [0, 1]) + oj(2, [2, 3]) + pj(1, [6, 7]) + sj(7, [0, 1])
-        + sj(7, [2, 3]) + oj(2, [4, 5]) + oj(2, [6, 7]) + oj(3, [0, 1]) + oj(3, [2, 3]) + oj(3, [4, 5])
+        xj(0) + w + pj(0, [0, 1]) + pj(0, [2, 3]) + pj(0, [4, 5]) + xj(1)
+        + pj(0, [6, 7]) + xj(2) + xj(3) + sj(0) + xj(4) + sj(1)
+        + sj(2) + xj(5) + oj(0, [0, 1]) + sj(3) + oj(0, [2, 3]) + sj(4)
+        + pj(1, [0, 1]) + oj(0, [4, 5]) + oj(0, [6, 7]) + sj(5, [0, 1]) + oj(1, [0, 1]) + xj(6)
+        + xj(7) + oj(1, [2, 3]) + sj(5, [2, 3]) + oj(1, [4, 5]) + pj(1, [2, 3]) + pj(1, [4, 5])
+        + sj(6, [0, 1]) + oj(1, [6, 7]) + oj(2, [0, 1]) + oj(2, [2, 3]) + sj(6, [2, 3]) + pj(1, [6, 7])
+        + sj(7) + oj(2, [4, 5]) + oj(2, [6, 7]) + oj(3, [0, 1]) + oj(3, [2, 3]) + oj(3, [4, 5])
         + oj(3, [6, 7])
     )
 
@@ -92,16 +91,16 @@ def tile_causalselfattention_pa_t_kernel(tc, x, wk_bytes, wk_scale, pk_w, pk_b, 
         bias_bf = keep.tile([P, 4, 4], BF16, name="bias_bf", align_bytes=64)
         bias = keep.tile([P, 16], F32, name="bias", align_bytes=64)
         load_p(0, 0, 0)
-        load_x(1, 1)
-        load_x(2, 1)
-        load_x(3, 1)
         load_p(0, 0, 1)
         load_p(0, 1, 0)
+        load_x(1, 1)
+        load_p(0, 1, 1)
+        load_x(2, 1)
+        load_x(3, 1)
         load_x(4, 1)
         load_x(5, 1)
-        load_x(6, 1)
-        load_p(0, 1, 1)
         load_p(1, 0, 0)
+        load_x(6, 1)
         nc.sync.dma_start(out=bias_bf[:], in_=pk_b.rearrange("c (q p j) -> p (c q) j", q=2, j=4))
         load_x(7, 1)
         load_p(1, 0, 1)
@@ -114,8 +113,6 @@ def tile_causalselfattention_pa_t_kernel(tc, x, wk_bytes, wk_scale, pk_w, pk_b, 
         nc.scalar.activation(out=warm2[:], in_=warm[:], func=IDENT)
         ident = keep.tile([P, P], F32, name="ident", align_bytes=64)
         make_identity(nc, ident[:])
-        ident_bf = keep.tile([P, P], BF16, name="ident_bf", align_bytes=64)
-        nc.gpsimd.tensor_copy(out=ident_bf[:], in_=ident[:])
         nc.gpsimd.tensor_copy(out=bias[:], in_=bias_bf[:].rearrange("p a j -> p (a j)"))
 
         wv = keep.tile([P, 4, C], BF16, name="wv", align_bytes=64)
@@ -132,21 +129,22 @@ def tile_causalselfattention_pa_t_kernel(tc, x, wk_bytes, wk_scale, pk_w, pk_b, 
         grouped = {}
         due = []
         count = [0, 0]
+        evac_count = {}
         words = {}
 
-        def evac_engine():
-            e = EVAC[count[1] % len(EVAC)]
-            count[1] += 1
-            return e
+        def evac_engine(kind):
+            n = evac_count.get(kind, 0)
+            evac_count[kind] = n + 1
+            return EVAC[kind][n % len(EVAC[kind])]
 
-        def copy_out(out_, in_):
-            if evac_engine() == "S":
+        def copy_out(kind, out_, in_):
+            if evac_engine(kind) == "S":
                 nc.scalar.copy(out=out_, in_=in_)
             else:
                 nc.vector.tensor_copy(out=out_, in_=in_)
 
-        def later(fn):
-            due.append((count[0] + QDELAY, fn))
+        def later(fn, delay=QDELAY):
+            due.append((count[0] + delay, fn))
 
         def quant(codes, scales, src):
             nc.vector.quantize_mx(out=codes[:].bitcast(FP8X4), scales=scales[:], in_=src[:])
@@ -177,23 +175,28 @@ def tile_causalselfattention_pa_t_kernel(tc, x, wk_bytes, wk_scale, pk_w, pk_b, 
             bk = bank("t")
             for n in range(4):
                 nc.tensor.transpose(bk[:, n * P:(n + 1) * P], words[job][n], ident[:])
-            copy_out(dst.bitcast(F32).rearrange("p (g m u) -> p g m u", g=2, u=2),
+            copy_out("t", dst.bitcast(F32).rearrange("p (g m u) -> p g m u", g=2, u=2),
                      bk[:].rearrange("p (g u m) -> p g m u", g=2, u=2))
 
         def do_w(a):
-            bk = psum.tile([P, 2, 4, P], BF16, name="bank")
+            bk = bank("w")
             for i2 in range(2):
-                for t in range(4):
-                    nc.tensor.transpose(bk[:, i2, t, :], wv[:, 2 * a + i2, t:C:4], ident_bf[:])
+                ww = wv[:, 2 * a + i2, :].bitcast(F32)
+                for u in range(2):
+                    n = 2 * i2 + u
+                    nc.tensor.transpose(bk[:, n * P:(n + 1) * P], ww[:, u:256:2], ident[:])
+            vals = bk[:].bitcast(BF16)
             for i2 in range(2):
                 base = (2 * a + i2) * 512
                 nc.vector.tensor_tensor(
-                    out=wg[:, base:base + 512].rearrange("p (r t) -> p r t", t=4),
-                    in0=bk[:, i2, :, :].rearrange("p t r -> p r t"),
-                    in1=ws[:].unsqueeze(1).to_broadcast([P, P, 4]),
+                    out=wg[:, base:base + 512].rearrange("p (r u e) -> p r u e", u=2, e=2),
+                    in0=vals[:, i2 * 512:(i2 + 1) * 512].rearrange("p (u r e) -> p r u e", u=2, e=2),
+                    in1=ws[:].rearrange("p (u e) -> p u e", u=2).unsqueeze(1).to_broadcast([P, P, 2, 2]),
                     op=MULT)
-            if a == 1:
-                later(lambda: quant(wcodes, wscales, wg))
+            later(lambda: nc.vector.quantize_mx(
+                out=wcodes[:, a * 256:(a + 1) * 256].bitcast(FP8X4),
+                scales=wscales[:, a * 256:(a + 1) * 256],
+                in_=wg[:, a * 1024:(a + 1) * 1024]), 1)
 
         def do_x(i, a):
             if a == 0:
@@ -229,7 +232,7 @@ def tile_causalselfattention_pa_t_kernel(tc, x, wk_bytes, wk_scale, pk_w, pk_b, 
                     rhs=wcodes[:, h * P:(h + 1) * P].bitcast(FP8X4),
                     rhs_scale=wscales[:, h * P:(h + 1) * P],
                     start=True, stop=True)
-            copy_out(g[:, h * 512:(h + 1) * 512].rearrange("p (n t) -> p n t", t=4),
+            copy_out("s", g[:, h * 512:(h + 1) * 512].rearrange("p (n t) -> p n t", t=4),
                      bk[:].rearrange("p (t n) -> p n t", t=4))
             if h == 3:
                 kcodes[i] = work.tile([P, C], U32, name="kcodes", bufs=8, align_bytes=64)
@@ -277,10 +280,10 @@ def tile_causalselfattention_pa_t_kernel(tc, x, wk_bytes, wk_scale, pk_w, pk_b, 
                 store(nc.sync, 0, 2, 2, 4)
                 store(nc.scalar, 2, 4, 2, 4)
             else:
-                emit(evac_engine(), 0, NH)
-                if pair == 3 and q == 1:
-                    if jj == 1:
-                        store(nc.sync, 0, NH, 0, 2)
+                emit(evac_engine("o"), 0, NH)
+                if pair == 3 or (pair == 2 and q == 1):
+                    if jj % 2 == 1:
+                        store(nc.sync, 0, NH, jj - 1, jj + 1)
                 elif jj == 3:
                     store(nc.sync, 0, NH, 0, 4)
 
@@ -300,5 +303,7 @@ def tile_causalselfattention_pa_t_kernel(tc, x, wk_bytes, wk_scale, pk_w, pk_b, 
             else:
                 do_o(job[1], job[2])
             count[0] += 1
-            while due and due[0][0] <= count[0]:
-                due.pop(0)[1]()
+            ready = [d for d in due if d[0] <= count[0]]
+            for d in ready:
+                due.remove(d)
+                d[1]()

from contextlib import ExitStack

import concourse.mybir as mybir
from concourse.masks import make_identity

B, T, C, NH, NC = 2, 2048, 512, 4, 2
D = C // NH
N = T // NC
FLOPS = 2 * B * T * C * C + 2 * B * T * N * C

F32 = mybir.dt.float32
BF16 = mybir.dt.bfloat16
U32 = mybir.dt.uint32
U8 = mybir.dt.uint8
FP8 = mybir.dt.float8_e4m3fn
FP8X4 = mybir.dt.float8_e4m3fn_x4
ADD = mybir.AluOpType.add
MULT = mybir.AluOpType.mult
IDENT = mybir.ActivationFunctionType.Identity
P = 128

EVAC = {"t": "SVS", "s": "SSSV", "o": "SSVSSSV"}
QDELAY = 3
LEAD = 10
DEINT_X = [6,7]
DEINT_P = [8,9,10,11,12,13,14,15]
DEINT_ENGINE = "V"


def build_schedule():
    def xj(i):
        return [("X", i, 0), ("X", i, 1)]

    def pj(c, js):
        return [("P", c, j) for j in js]

    def sj(i, hs=(0, 1, 2, 3)):
        return [("S", i, h) for h in hs]

    def oj(pair, js):
        return [("O", pair, j) for j in js]

    w = [("W", 0, 0), ("W", 1, 0)]
    return (
        xj(0) + w + pj(0, [0, 1]) + pj(0, [2, 3]) + pj(0, [4, 5]) + xj(1)
        + pj(0, [6, 7]) + xj(2) + xj(3) + sj(0) + xj(4) + sj(1)
        + sj(2) + xj(5) + oj(0, [0, 1]) + sj(3) + oj(0, [2, 3]) + sj(4)
        + pj(1, [0, 1]) + oj(0, [4, 5]) + oj(0, [6, 7]) + sj(5, [0, 1]) + oj(1, [0, 1]) + xj(6)
        + xj(7) + oj(1, [2, 3]) + sj(5, [2, 3]) + oj(1, [4, 5]) + pj(1, [2, 3]) + pj(1, [4, 5])
        + sj(6, [0, 1]) + oj(1, [6, 7]) + oj(2, [0, 1]) + oj(2, [2, 3]) + sj(6, [2, 3]) + pj(1, [6, 7])
        + sj(7) + oj(2, [4, 5]) + oj(2, [6, 7]) + oj(3, [0, 1]) + oj(3, [2, 3]) + oj(3, [4, 5])
        + oj(3, [6, 7])
    )


def tile_causalselfattention_pa_t_kernel(tc, x, wk_bytes, wk_scale, pk_w, pk_b, out):
    nc = tc.nc
    with ExitStack() as ctx:
        keep = ctx.enter_context(tc.tile_pool(name="keep", bufs=1))
        work = ctx.enter_context(tc.tile_pool(name="work", bufs=3))
        psum = ctx.enter_context(tc.psum_pool(name="psum", bufs=8))
        ctx.enter_context(tc.manual_schedule())

        wb = keep.tile([P, 4, C], U8, name="wb", align_bytes=64)
        nc.sync.dma_start(out=wb[:], in_=wk_bytes.rearrange("(i r) k -> r i k", r=P))
        ws = keep.tile([P, 4], F32, name="ws", align_bytes=64)
        nc.scalar.dma_start(out=ws[:], in_=wk_scale.rearrange("o (p t) -> p (o t)", t=4))

        xraw = {}
        praw = {}

        def load_x(i, pieces):
            pair, u = divmod(i, 2)
            c, b = divmod(pair, 2)
            r0 = c * N + u * 512
            t = keep.tile([P, 4, C], BF16, name="xraw%d" % i, align_bytes=64)
            src = x[b, r0:r0 + 512, :].rearrange("(m t) k -> m t k", t=4)
            n = 4 // pieces
            for s in range(pieces):
                nc.sync.dma_start(out=t[:, s * n:(s + 1) * n, :], in_=src[:, s * n:(s + 1) * n, :])
            xraw[i] = t

        def load_p(c, q, half):
            if (c, q) not in praw:
                praw[(c, q)] = keep.tile([P, 4, N], BF16, name="praw%d%d" % (c, q), align_bytes=64)
            src = pk_w[c, q * 512:(q + 1) * 512, :].rearrange("(m j) k -> m j k", j=4)
            rows = slice(2 * half, 2 * half + 2)
            nc.sync.dma_start(out=praw[(c, q)][:, rows, :], in_=src[:, rows, :])

        load_x(0, 2)
        bias_bf = keep.tile([P, 4, 4], BF16, name="bias_bf", align_bytes=64)
        bias = keep.tile([P, 16], F32, name="bias", align_bytes=64)
        load_p(0, 0, 0)
        load_p(0, 0, 1)
        load_p(0, 1, 0)
        load_x(1, 1)
        load_p(0, 1, 1)
        load_x(2, 1)
        load_x(3, 1)
        load_x(4, 1)
        load_x(5, 1)
        load_p(1, 0, 0)
        load_x(6, 1)
        nc.sync.dma_start(out=bias_bf[:], in_=pk_b.rearrange("c (q p j) -> p (c q) j", q=2, j=4))
        load_x(7, 1)
        load_p(1, 0, 1)
        load_p(1, 1, 0)
        load_p(1, 1, 1)

        warm = keep.tile([P, 1], F32, name="warm")
        warm2 = keep.tile([P, 1], F32, name="warm2")
        nc.vector.memset(warm[:], 0.0)
        nc.scalar.activation(out=warm2[:], in_=warm[:], func=IDENT)
        ident = keep.tile([P, P], F32, name="ident", align_bytes=64)
        make_identity(nc, ident[:])
        nc.gpsimd.tensor_copy(out=bias[:], in_=bias_bf[:].rearrange("p a j -> p (a j)"))

        wv = keep.tile([P, 4, C], BF16, name="wv", align_bytes=64)
        nc.vector.tensor_copy(out=wv[:, 0:2, :].rearrange("p i k -> p (i k)"),
                              in_=wb[:, 0:2, :].rearrange("p i k -> p (i k)").bitcast(FP8))
        nc.scalar.copy(out=wv[:, 2:4, :].rearrange("p i k -> p (i k)"),
                       in_=wb[:, 2:4, :].rearrange("p i k -> p (i k)").bitcast(FP8))

        wg = keep.tile([P, C * 4], BF16, name="wg", align_bytes=64)
        wcodes = keep.tile([P, C], U32, name="wcodes", align_bytes=64)
        wscales = keep.tile([P, C], U8, name="wscales", align_bytes=64)

        xcodes, xscales, pcodes, pscales, kcodes, kscales, otiles = {}, {}, {}, {}, {}, {}, {}
        grouped = {}
        due = []
        count = [0, 0]
        evac_count = {}
        words = {}

        def evac_engine(kind):
            n = evac_count.get(kind, 0)
            evac_count[kind] = n + 1
            return EVAC[kind][n % len(EVAC[kind])]

        def copy_out(kind, out_, in_):
            if evac_engine(kind) == "S":
                nc.scalar.copy(out=out_, in_=in_)
            else:
                nc.vector.tensor_copy(out=out_, in_=in_)

        def later(fn, delay=QDELAY):
            due.append((count[0] + delay, fn))

        def quant(codes, scales, src):
            nc.vector.quantize_mx(out=codes[:].bitcast(FP8X4), scales=scales[:], in_=src[:])

        def raw_words(kind, i, a):
            if kind == "X":
                return xraw[i][:, 2 * a:2 * a + 2, :].rearrange("p s k -> p (s k)").bitcast(F32)
            return praw[(i, a // 4)][:, a % 4, :].bitcast(F32)

        def deinterleave(job):
            kind = job[0]
            if job in words:
                return
            if (kind == "X" and job[1] in DEINT_X) or (kind == "P" and (job[1] * 8 + job[2]) in DEINT_P):
                d = work.tile([P, 4, P], F32, name="deint", bufs=10, align_bytes=64)
                eng = nc.vector if DEINT_ENGINE == "V" else nc.gpsimd
                eng.tensor_copy(out=d[:].rearrange("p (g u) m -> p g u m", g=2),
                                in_=raw_words(*job).rearrange("p (g m u) -> p g u m", g=2, u=2))
                words[job] = [d[:, n, :] for n in range(4)]
            elif kind in ("X", "P"):
                r = raw_words(*job)
                words[job] = [r[:, 256 * g + u:256 * (g + 1):2] for g in range(2) for u in range(2)]

        def bank(name):
            return psum.tile([P, 512], F32, name="bank")

        def turn(job, dst):
            bk = bank("t")
            for n in range(4):
                nc.tensor.transpose(bk[:, n * P:(n + 1) * P], words[job][n], ident[:])
            copy_out("t", dst.bitcast(F32).rearrange("p (g m u) -> p g m u", g=2, u=2),
                     bk[:].rearrange("p (g u m) -> p g m u", g=2, u=2))

        def do_w(a):
            bk = bank("w")
            for i2 in range(2):
                ww = wv[:, 2 * a + i2, :].bitcast(F32)
                for u in range(2):
                    n = 2 * i2 + u
                    nc.tensor.transpose(bk[:, n * P:(n + 1) * P], ww[:, u:256:2], ident[:])
            vals = bk[:].bitcast(BF16)
            for i2 in range(2):
                base = (2 * a + i2) * 512
                nc.vector.tensor_tensor(
                    out=wg[:, base:base + 512].rearrange("p (r u e) -> p r u e", u=2, e=2),
                    in0=vals[:, i2 * 512:(i2 + 1) * 512].rearrange("p (u r e) -> p r u e", u=2, e=2),
                    in1=ws[:].rearrange("p (u e) -> p u e", u=2).unsqueeze(1).to_broadcast([P, P, 2, 2]),
                    op=MULT)
            later(lambda: nc.vector.quantize_mx(
                out=wcodes[:, a * 256:(a + 1) * 256].bitcast(FP8X4),
                scales=wscales[:, a * 256:(a + 1) * 256],
                in_=wg[:, a * 1024:(a + 1) * 1024]), 1)

        def do_x(i, a):
            if a == 0:
                grouped[("X", i)] = work.tile([P, 2048], BF16, name="xg", align_bytes=64)
            g = grouped[("X", i)]
            turn(("X", i, a), g[:, a * 1024:(a + 1) * 1024])
            if a == 1:
                xcodes[i] = work.tile([P, C], U32, name="xcodes", bufs=6, align_bytes=64)
                xscales[i] = work.tile([P, C], U8, name="xscales", bufs=6, align_bytes=64)
                later(lambda: quant(xcodes[i], xscales[i], g))

        def do_p(c, j):
            key = (c, j // 2)
            if j % 2 == 0:
                grouped[("P",) + key] = work.tile([P, 2048], BF16, name="pg", align_bytes=64)
            g = grouped[("P",) + key]
            turn(("P", c, j), g[:, (j % 2) * 1024:(j % 2 + 1) * 1024])
            if j % 2 == 1:
                pcodes[key] = keep.tile([P, 512], U32, name="pcodes%d%d" % key, align_bytes=64)
                pscales[key] = keep.tile([P, 512], U8, name="pscales%d%d" % key, align_bytes=64)
                later(lambda: quant(pcodes[key], pscales[key], g))

        def do_s(i, h):
            if h == 0:
                grouped[("K", i)] = work.tile([P, 2048], BF16, name="kg", align_bytes=64)
            g = grouped[("K", i)]
            bk = bank("s")
            for t in range(4):
                nc.tensor.matmul_mx(
                    out=bk[:, t * P:(t + 1) * P],
                    lhsT=xcodes[i][:, t * P:(t + 1) * P].bitcast(FP8X4),
                    lhsT_scale=xscales[i][:, t * P:(t + 1) * P],
                    rhs=wcodes[:, h * P:(h + 1) * P].bitcast(FP8X4),
                    rhs_scale=wscales[:, h * P:(h + 1) * P],
                    start=True, stop=True)
            copy_out("s", g[:, h * 512:(h + 1) * 512].rearrange("p (n t) -> p n t", t=4),
                     bk[:].rearrange("p (t n) -> p n t", t=4))
            if h == 3:
                kcodes[i] = work.tile([P, C], U32, name="kcodes", bufs=8, align_bytes=64)
                kscales[i] = work.tile([P, C], U8, name="kscales", bufs=8, align_bytes=64)
                later(lambda: quant(kcodes[i], kscales[i], g))

        def do_o(pair, j):
            c, b = divmod(pair, 2)
            q, jj = divmod(j, 4)
            if jj == 0:
                otiles[(pair, q)] = work.tile([P, NH, 4, D], F32, name="o", align_bytes=64)
            o = otiles[(pair, q)]
            bk = bank("o")
            s0 = (j % 2) * 256
            key = (c, j // 2)
            for u in range(2):
                cols = slice(s0 + u * P, s0 + (u + 1) * P)
                nc.tensor.matmul_mx(
                    out=bk[:],
                    lhsT=pcodes[key][:, cols].bitcast(FP8X4),
                    lhsT_scale=pscales[key][:, cols],
                    rhs=kcodes[2 * pair + u][:].bitcast(FP8X4),
                    rhs_scale=kscales[2 * pair + u][:],
                    start=(u == 0), stop=(u == 1))
            bcol = bias[:, (2 * c + q) * 4 + jj:(2 * c + q) * 4 + jj + 1]
            src = bk[:].rearrange("p (h d) -> p h d", h=NH)
            last = pair == 3 and j == 7

            def emit(e, h0, h1):
                if e == "S":
                    nc.scalar.activation(out=o[:, h0:h1, jj, :], in_=src[:, h0:h1, :], func=IDENT, bias=bcol)
                else:
                    nc.vector.tensor_scalar(out=o[:, h0:h1, jj, :], in0=src[:, h0:h1, :], scalar1=bcol, scalar2=None, op0=ADD)

            r0 = c * N + q * 512

            def store(eng, h0, h1, j0, j1):
                dst = out[b, h0:h1, r0:r0 + 512, :].rearrange("h (p j) d -> p h j d", j=4)[:, :, j0:j1, :]
                eng.dma_start(out=dst.rearrange("p h j d -> p h (j d)"),
                              in_=o[:, h0:h1, j0:j1, :].rearrange("p h j d -> p h (j d)"))

            if last:
                emit("V", 0, 2)
                emit("S", 2, 4)
                store(nc.sync, 0, 2, 2, 4)
                store(nc.scalar, 2, 4, 2, 4)
            else:
                emit(evac_engine("o"), 0, NH)
                if pair == 3 or (pair == 2 and q == 1):
                    if jj % 2 == 1:
                        store(nc.sync, 0, NH, jj - 1, jj + 1)
                elif jj == 3:
                    store(nc.sync, 0, NH, 0, 4)

        schedule = build_schedule()
        for n, job in enumerate(schedule):
            for ahead in schedule[n:n + LEAD + 1]:
                deinterleave(ahead)
            kind = job[0]
            if kind == "W":
                do_w(job[1])
            elif kind == "X":
                do_x(job[1], job[2])
            elif kind == "P":
                do_p(job[1], job[2])
            elif kind == "S":
                do_s(job[1], job[2])
            else:
                do_o(job[1], job[2])
            count[0] += 1
            ready = [d for d in due if d[0] <= count[0]]
            for d in ready:
                due.remove(d)
                d[1]()
